import numpy as np
import ml_dtypes


def mxq(x, axis, fmt="e4m3"):
    dtype, down = {"e4m3": (ml_dtypes.float8_e4m3fn, 7), "e5m2": (ml_dtypes.float8_e5m2, 14)}[fmt]
    v = np.moveaxis(np.asarray(x, np.float32).astype(ml_dtypes.bfloat16).astype(np.float64), axis, -1)
    blocks = v.reshape(v.shape[:-1] + (-1, 32))
    amax = np.abs(blocks).max(-1, keepdims=True)
    byte = np.maximum(np.where(amax > 0, np.frexp(amax)[1] - 1 + 127, 0) - down, 1)
    scale = np.exp2(byte - 127.0)
    codes = (blocks / scale).astype(np.float32).astype(dtype).astype(np.float64)
    return np.moveaxis((codes * scale).reshape(v.shape), -1, axis)


WIDE = False


def mx_kscale(k):
    if not WIDE:
        return np.ones(k)
    levels = np.array([10, -10, 5, -5, 0])
    a = np.random.permutation(np.resize(levels, k // 512 * 4)).reshape(k // 512, 4)
    idx = np.arange(k)
    return np.exp2(a[idx // 512, idx % 128 // 32])


BF16 = ml_dtypes.bfloat16


def bf(x):
    return np.asarray(x, np.float32).astype(BF16)


def f64(x):
    return np.asarray(x).astype(np.float64)


E2M1 = np.array([0.0, 0.5, 1.0, 1.5, 2.0, 3.0, 4.0, 6.0, -0.0, -0.5, -1.0, -1.5, -2.0, -3.0, -4.0, -6.0])


def pack_weight(w, fmt):
    k, n = w.shape
    w = f64(bf(w)).reshape(k // 32, 32, n)
    amax = np.abs(w).max(1)
    if fmt == "e4m3":
        byte = np.frexp(amax)[1] - 1 + 127 - 7
    else:
        mant, ex = np.frexp(amax / 6.0)
        byte = np.where(mant > 0.5, ex, ex - 1) + 127
    byte = np.clip(np.where(amax > 0, byte, 1), 1, 254)
    scaled = (w * np.exp2(127.0 - byte)[:, None, :]).reshape(k, n).astype(np.float32)
    by_word = np.ascontiguousarray(scaled.reshape(k // 512, 128, 4, n).transpose(0, 1, 3, 2))
    if fmt == "e4m3":
        words = by_word.astype(ml_dtypes.float8_e4m3fn).view(np.uint8)
    else:
        c = by_word.astype(ml_dtypes.float4_e2m1fn).view(np.uint8) & 0xF
        words = c[..., 0::2] | (c[..., 1::2] << 4)
    return np.ascontiguousarray(words), np.ascontiguousarray(byte.astype(np.uint8).reshape(k // 512, 16, n))


def unpack_weight(words, scales, fmt):
    g, p, n, _ = words.shape
    if fmt == "e4m3":
        vals = np.ascontiguousarray(words).view(ml_dtypes.float8_e4m3fn).astype(np.float64)
    else:
        nib = np.empty((g, p, n, 4), np.uint8)
        nib[..., 0::2] = words & 0xF
        nib[..., 1::2] = words >> 4
        vals = E2M1[nib]
    vals = vals * np.repeat(np.exp2(scales.astype(np.float64) - 127.0), 8, axis=1)[..., None]
    return vals.transpose(0, 1, 3, 2).reshape(g * 512, n)


N, FIN, FD, F1, F2, F3, E = 512, 2048, 8192, 256, 256, 128, 2


def elu(v):
    return np.where(v > 0.0, v, np.exp(np.minimum(v, 0.0)) - 1.0)


def setup_inputs():
    s = mx_kscale(FD)
    k = mx_kscale(N)
    t = np.where(np.arange(E) % 2 == 0, k.max(), k.min())
    x = bf(elu(np.random.standard_normal((N, FD))) * s)
    adjacency_matrix = bf(np.random.uniform(size=(E, N, N)) * 0.5 / np.sqrt(N) / t[:, None, None])
    W1 = bf(np.random.standard_normal((E, FD, F1)) / np.sqrt(FD) / s[:, None] * t[:, None, None])
    b1 = bf(np.random.standard_normal(F1) * 0.3)
    Wr1_words, Wr1_scales = pack_weight(np.random.standard_normal((FD, F1)) * 0.3 / np.sqrt(FD) / s[:, None], "e4m3")
    return {
        "x": x,
        "adjacency_matrix": adjacency_matrix,
        "W1": W1,
        "b1": b1,
        "Wr1_words": Wr1_words,
        "Wr1_scales": Wr1_scales,
    }


def reference(x, adjacency_matrix, W1, b1, Wr1_words, Wr1_scales):
    xq = mxq(f64(x), 1, "e4m3")
    support = xq @ mxq(f64(W1), 1, "e4m3")
    agg = (mxq(f64(adjacency_matrix), 2, "e4m3") @ mxq(support, 1, "e4m3")).sum(0)
    return agg + f64(b1) + (xq @ unpack_weight(Wr1_words, Wr1_scales, "e4m3"))

@@ -1,0 +1,250 @@
+from contextlib import ExitStack
+
+import concourse.mybir as mybir
+from concourse.masks import make_identity
+
+F32 = mybir.dt.float32
+BF16 = mybir.dt.bfloat16
+I32 = mybir.dt.int32
+U32 = mybir.dt.uint32
+U8 = mybir.dt.uint8
+FP8X4 = mybir.dt.float8_e4m3fn_x4
+ADD = mybir.AluOpType.add
+
+P = 128
+PACK = 4
+K_PASS = P * PACK
+NODES = 512
+FEATURES = 8192
+F_OUT = 256
+EDGE_TYPES = 2
+NODE_TILES = NODES // P
+PASSES = FEATURES // K_PASS
+ROUND = 2
+ROUNDS = PASSES // ROUND
+LEAD = 2
+W_COLS = EDGE_TYPES * F_OUT
+
+FLOPS = 2 * NODES * FEATURES * (W_COLS + F_OUT) + 2 * EDGE_TYPES * NODES * NODES * F_OUT
+
+
+def tile_fgg_pa_k_kernel(tc, x, adjacency_matrix, W1, b1, Wr1_words, Wr1_scales, out):
+    nc = tc.nc
+    with ExitStack() as ctx:
+        ctx.enter_context(tc.manual_schedule())
+        keep = ctx.enter_context(tc.tile_pool(name="keep", bufs=1))
+        raw = ctx.enter_context(tc.tile_pool(name="raw", bufs=4))
+        stage = ctx.enter_context(tc.tile_pool(name="stage", bufs=4))
+        sup_psum = ctx.enter_context(tc.psum_pool(name="sup_psum", bufs=1))
+        work_psum = ctx.enter_context(tc.psum_pool(name="work_psum", bufs=4))
+
+        x_view = x.rearrange("(t p) k -> p t k", p=P)
+        adj_view = adjacency_matrix.rearrange("e (t p) m -> p (e t) m", p=P)
+        w1_view = W1.rearrange("e (g p j) w -> e g p (j w)", p=P, j=PACK)
+        wr_view = Wr1_words.rearrange("g p n t -> p g (n t)")
+        out_view = out.rearrange("(t p) f -> t p f", p=P)
+
+        ident_f32 = keep.tile([P, P], F32)
+        ident_bf16 = keep.tile([P, P], BF16)
+        xq_codes = keep.tile([P, PASSES * NODES], U32, align_bytes=64)
+        xq_scales = keep.tile([P, PASSES * NODES], U8, align_bytes=64)
+        wr_codes = keep.tile([P, PASSES, F_OUT], U32, align_bytes=64)
+        wr_scales = keep.tile([P, PASSES, F_OUT], U8, align_bytes=64)
+        adj_raw = keep.tile([P, EDGE_TYPES * NODE_TILES, NODES], BF16)
+        adj_grouped = keep.tile([P, EDGE_TYPES, NODES, PACK], BF16, align_bytes=64)
+        adjq_codes = keep.tile([P, EDGE_TYPES * NODES], U32, align_bytes=64)
+        adjq_scales = keep.tile([P, EDGE_TYPES * NODES], U8, align_bytes=64)
+        sup_rows = keep.tile([P, NODE_TILES, W_COLS], BF16)
+        sup_grouped = keep.tile([P, W_COLS, PACK], BF16, align_bytes=64)
+        supq_codes = keep.tile([P, W_COLS], U32, align_bytes=64)
+        supq_scales = keep.tile([P, W_COLS], U8, align_bytes=64)
+        bias_bf16 = keep.tile([P, F_OUT], BF16)
+        bias_f32 = keep.tile([P, F_OUT], F32)
+        result = keep.tile([P, NODE_TILES, F_OUT], F32)
+
+        support = [sup_psum.tile([P, W_COLS], F32, name="support%d" % t) for t in range(NODE_TILES)]
+
+        x_raw = {}
+        x_grouped = {}
+        w_raw = {}
+        w_grouped = {}
+        wq_codes = {}
+        wq_scales = {}
+
+        def load_x(r):
+            x_raw[r] = raw.tile([P, NODE_TILES, ROUND * K_PASS], BF16, name="x_raw")
+            nc.sync.dma_start(out=x_raw[r][:], in_=x_view[:, :, r * ROUND * K_PASS : (r + 1) * ROUND * K_PASS])
+
+        def load_w(g):
+            w_raw[g] = raw.tile([P, EDGE_TYPES, PACK * F_OUT], BF16, name="w_raw")
+            for e in range(EDGE_TYPES):
+                nc.sync.dma_start(out=w_raw[g][:, e, :], in_=w1_view[e, g])
+
+        def transpose_x(r):
+            words = x_raw[r][:].bitcast(F32)
+            x_grouped[r] = stage.tile([P, ROUND, NODES, PACK], BF16, name="x_grouped", align_bytes=64)
+            grouped_words = x_grouped[r][:].bitcast(F32)
+            for i in range(ROUND):
+                for half in range(2):
+                    xt = work_psum.tile([P, 2, 2 * P], F32, tag="work")
+                    for u in range(2):
+                        for a in range(2):
+                            nc.tensor.transpose(
+                                xt[:, u, a * P : (a + 1) * P],
+                                words[:, 2 * half + a, 256 * i + u : 256 * (i + 1) : 2],
+                                ident_f32[:],
+                            )
+                    nc.scalar.copy(
+                        out=grouped_words[:, i, 2 * P * half : 2 * P * (half + 1), :],
+                        in_=xt[:].rearrange("p u n -> p n u"),
+                    )
+
+        def quantise_x(r, i):
+            g = ROUND * r + i
+            nc.vector.quantize_mx(
+                out=xq_codes[:, g * NODES : (g + 1) * NODES].bitcast(FP8X4),
+                scales=xq_scales[:, g * NODES : (g + 1) * NODES],
+                in_=x_grouped[r][:, i].rearrange("p n t -> p (n t)"),
+            )
+
+        def regroup_w(g):
+            w_grouped[g] = stage.tile([P, EDGE_TYPES, F_OUT * PACK], BF16, name="w_grouped", align_bytes=64)
+            for e in range(EDGE_TYPES):
+                src = w_raw[g][:, e, :].rearrange("p (j c i) -> p c j i", j=PACK, i=4)
+                dst = w_grouped[g][:, e, :].rearrange("p (c i j) -> p c j i", j=PACK, i=4)
+                if e == 1 and g % 2 == 1:
+                    nc.scalar.copy(out=dst, in_=src)
+                else:
+                    nc.vector.tensor_copy(out=dst, in_=src)
+
+        def quantise_w(g):
+            wq_codes[g] = stage.tile([P, W_COLS], U32, name="wq_codes", align_bytes=64)
+            wq_scales[g] = stage.tile([P, W_COLS], U8, name="wq_scales", align_bytes=64)
+            nc.vector.quantize_mx(
+                out=wq_codes[g][:].bitcast(FP8X4),
+                scales=wq_scales[g][:],
+                in_=w_grouped[g][:].rearrange("p e n -> p (e n)"),
+            )
+
+        def x_operand(g, t):
+            cols = slice(g * NODES + t * P, g * NODES + (t + 1) * P)
+            return xq_codes[:, cols].bitcast(FP8X4), xq_scales[:, cols]
+
+        def support_passes(g):
+            for t in range(NODE_TILES):
+                codes, scales = x_operand(g, t)
+                nc.tensor.matmul_mx(
+                    out=support[t][:],
+                    lhsT=codes,
+                    lhsT_scale=scales,
+                    rhs=wq_codes[g][:].bitcast(FP8X4),
+                    rhs_scale=wq_scales[g][:],
+                    start=(g == 0),
+                    stop=(g == PASSES - 1),
+                )
+
+        make_identity(nc, ident_bf16[:])
+        make_identity(nc, ident_f32[:])
+        nc.vector.memset(wr_scales[:].rearrange("p g n -> p (g n)").bitcast(I32), 0)
+
+        nc.sync.dma_start(out=adj_raw[:], in_=adj_view)
+        for r in range(LEAD):
+            load_x(r)
+
+        for e in range(EDGE_TYPES):
+            for half in range(2):
+                at = work_psum.tile([P, 2, PACK, P], BF16, tag="work")
+                for a in range(2):
+                    for t in range(PACK):
+                        nc.tensor.transpose(
+                            at[:, a, t, :],
+                            adj_raw[:, e * NODE_TILES + 2 * half + a, t * P : (t + 1) * P],
+                            ident_bf16[:],
+                        )
+                dst = adj_grouped[:, e, 2 * P * half : 2 * P * (half + 1), :].rearrange("p (a r) t -> p a r t", a=2)
+                src = at[:].rearrange("p a t r -> p a r t")
+                if half == 0:
+                    nc.vector.tensor_copy(out=dst, in_=src)
+                else:
+                    nc.scalar.copy(out=dst, in_=src)
+        nc.vector.quantize_mx(
+            out=adjq_codes[:].bitcast(FP8X4),
+            scales=adjq_scales[:],
+            in_=adj_grouped[:].rearrange("p e n t -> p (e n t)"),
+        )
+
+        for r in range(LEAD):
+            transpose_x(r)
+        for i in range(ROUND):
+            quantise_x(0, i)
+        for r in range(ROUNDS):
+            for i in range(ROUND):
+                load_w(ROUND * r + i)
+            if r + LEAD < ROUNDS:
+                load_x(r + LEAD)
+            for i in range(ROUND):
+                regroup_w(ROUND * r + i)
+                if r + 1 < ROUNDS:
+                    quantise_x(r + 1, i)
+                quantise_w(ROUND * r + i)
+            if r + LEAD < ROUNDS:
+                transpose_x(r + LEAD)
+            for i in range(ROUND):
+                support_passes(ROUND * r + i)
+
+        for row in range(4):
+            nc.sync.dma_start(
+                out=wr_scales[row:P:32, :, :].bitcast(I32),
+                in_=Wr1_scales[:, row:16:4, :].rearrange("g q n -> q g n").bitcast(I32),
+            )
+        for c in range(4):
+            nc.sync.dma_start(
+                out=wr_codes[:, 4 * c : 4 * (c + 1), :].bitcast(I32),
+                in_=wr_view[:, 4 * c : 4 * (c + 1), :].bitcast(I32),
+            )
+        nc.sync.dma_start(out=bias_bf16[:], in_=b1.partition_broadcast(P))
+
+        total = [work_psum.tile([P, F_OUT], F32, tag="work", name="total%d" % t) for t in range(NODE_TILES)]
+        for g in range(PASSES):
+            for t in range(NODE_TILES):
+                codes, scales = x_operand(g, t)
+                nc.tensor.matmul_mx(
+                    out=total[t][:],
+                    lhsT=codes,
+                    lhsT_scale=scales,
+                    rhs=wr_codes[:, g, :].bitcast(FP8X4),
+                    rhs_scale=wr_scales[:, g, :],
+                    start=(g == 0),
+                    stop=False,
+                )
+        for t in range(NODE_TILES):
+            if t % 2 == 0:
+                nc.vector.tensor_copy(out=sup_rows[:, t, :], in_=support[t][:])
+            else:
+                nc.scalar.copy(out=sup_rows[:, t, :], in_=support[t][:])
+        nc.vector.tensor_copy(
+            out=sup_grouped[:].rearrange("p (c i) t -> p c t i", i=4),
+            in_=sup_rows[:].rearrange("p t (c i) -> p c t i", i=4),
+        )
+        nc.vector.tensor_copy(out=bias_f32[:], in_=bias_bf16[:])
+        nc.vector.quantize_mx(
+            out=supq_codes[:].bitcast(FP8X4),
+            scales=supq_scales[:],
+            in_=sup_grouped[:].rearrange("p c t -> p (c t)"),
+        )
+
+        for t in range(NODE_TILES):
+            for e in range(EDGE_TYPES):
+                n_cols = slice(e * NODES + t * P, e * NODES + (t + 1) * P)
+                f_cols = slice(e * F_OUT, (e + 1) * F_OUT)
+                nc.tensor.matmul_mx(
+                    out=total[t][:],
+                    lhsT=adjq_codes[:, n_cols].bitcast(FP8X4),
+                    lhsT_scale=adjq_scales[:, n_cols],
+                    rhs=supq_codes[:, f_cols].bitcast(FP8X4),
+                    rhs_scale=supq_scales[:, f_cols],
+                    start=False,
+                    stop=(e == EDGE_TYPES - 1),
+                )
+            nc.vector.tensor_tensor(out=result[:, t, :], in0=total[t][:], in1=bias_f32[:], op=ADD)
+            nc.sync.dma_start(out=out_view[t], in_=result[:, t, :])

@@ -34,7 +34,7 @@ def tile_fgg_pa_k_kernel(tc, x, adjacency_matrix, W1, b1, Wr1_words, Wr1_scales,
         ctx.enter_context(tc.manual_schedule())
         keep = ctx.enter_context(tc.tile_pool(name="keep", bufs=1))
         raw = ctx.enter_context(tc.tile_pool(name="raw", bufs=4))
-        stage = ctx.enter_context(tc.tile_pool(name="stage", bufs=4))
+        stage = ctx.enter_context(tc.tile_pool(name="stage", bufs=3))
         sup_psum = ctx.enter_context(tc.psum_pool(name="sup_psum", bufs=1))
         work_psum = ctx.enter_context(tc.psum_pool(name="work_psum", bufs=4))
 
@@ -82,16 +82,22 @@ def tile_fgg_pa_k_kernel(tc, x, adjacency_matrix, W1, b1, Wr1_words, Wr1_scales,
 
         def transpose_x(r):
             words = x_raw[r][:].bitcast(F32)
+            x_sorted = stage.tile([P, NODE_TILES, ROUND, 2, P], F32)
+            for t in range(NODE_TILES):
+                nc.scalar.copy(
+                    out=x_sorted[:, t],
+                    in_=words[:, t, :].rearrange("p (i q u) -> p i u q", i=ROUND, u=2),
+                )
             x_grouped[r] = stage.tile([P, ROUND, NODES, PACK], BF16, name="x_grouped", align_bytes=64)
             grouped_words = x_grouped[r][:].bitcast(F32)
-            for i in range(ROUND):
-                for half in range(2):
+            for half in range(2):
+                for i in range(ROUND):
                     xt = work_psum.tile([P, 2, 2 * P], F32, tag="work")
                     for u in range(2):
                         for a in range(2):
                             nc.tensor.transpose(
                                 xt[:, u, a * P : (a + 1) * P],
-                                words[:, 2 * half + a, 256 * i + u : 256 * (i + 1) : 2],
+                                x_sorted[:, 2 * half + a, i, u, :],
                                 ident_f32[:],
                             )
                     nc.scalar.copy(
@@ -112,10 +118,7 @@ def tile_fgg_pa_k_kernel(tc, x, adjacency_matrix, W1, b1, Wr1_words, Wr1_scales,
             for e in range(EDGE_TYPES):
                 src = w_raw[g][:, e, :].rearrange("p (j c i) -> p c j i", j=PACK, i=4)
                 dst = w_grouped[g][:, e, :].rearrange("p (c i j) -> p c j i", j=PACK, i=4)
-                if e == 1 and g % 2 == 1:
-                    nc.scalar.copy(out=dst, in_=src)
-                else:
-                    nc.vector.tensor_copy(out=dst, in_=src)
+                nc.vector.tensor_copy(out=dst, in_=src)
 
         def quantise_w(g):
             wq_codes[g] = stage.tile([P, W_COLS], U32, name="wq_codes", align_bytes=64)

@@ -24,6 +24,8 @@ ROUND = 2
 ROUNDS = PASSES // ROUND
 LEAD = 2
 W_COLS = EDGE_TYPES * F_OUT
+WR_CHUNK = 4
+WR_CHUNKS = PASSES // WR_CHUNK
 
 FLOPS = 2 * NODES * FEATURES * (W_COLS + F_OUT) + 2 * EDGE_TYPES * NODES * NODES * F_OUT
 
@@ -34,7 +36,7 @@ def tile_fgg_pa_k_kernel(tc, x, adjacency_matrix, W1, b1, Wr1_words, Wr1_scales,
         ctx.enter_context(tc.manual_schedule())
         keep = ctx.enter_context(tc.tile_pool(name="keep", bufs=1))
         raw = ctx.enter_context(tc.tile_pool(name="raw", bufs=4))
-        stage = ctx.enter_context(tc.tile_pool(name="stage", bufs=3))
+        stage = ctx.enter_context(tc.tile_pool(name="stage", bufs=4))
         sup_psum = ctx.enter_context(tc.psum_pool(name="sup_psum", bufs=1))
         work_psum = ctx.enter_context(tc.psum_pool(name="work_psum", bufs=4))
 
@@ -82,22 +84,16 @@ def tile_fgg_pa_k_kernel(tc, x, adjacency_matrix, W1, b1, Wr1_words, Wr1_scales,
 
         def transpose_x(r):
             words = x_raw[r][:].bitcast(F32)
-            x_sorted = stage.tile([P, NODE_TILES, ROUND, 2, P], F32)
-            for t in range(NODE_TILES):
-                nc.scalar.copy(
-                    out=x_sorted[:, t],
-                    in_=words[:, t, :].rearrange("p (i q u) -> p i u q", i=ROUND, u=2),
-                )
             x_grouped[r] = stage.tile([P, ROUND, NODES, PACK], BF16, name="x_grouped", align_bytes=64)
             grouped_words = x_grouped[r][:].bitcast(F32)
-            for half in range(2):
-                for i in range(ROUND):
+            for i in range(ROUND):
+                for half in range(2):
                     xt = work_psum.tile([P, 2, 2 * P], F32, tag="work")
                     for u in range(2):
                         for a in range(2):
                             nc.tensor.transpose(
                                 xt[:, u, a * P : (a + 1) * P],
-                                x_sorted[:, 2 * half + a, i, u, :],
+                                words[:, 2 * half + a, 256 * i + u : 256 * (i + 1) : 2],
                                 ident_f32[:],
                             )
                     nc.scalar.copy(
@@ -118,7 +114,10 @@ def tile_fgg_pa_k_kernel(tc, x, adjacency_matrix, W1, b1, Wr1_words, Wr1_scales,
             for e in range(EDGE_TYPES):
                 src = w_raw[g][:, e, :].rearrange("p (j c i) -> p c j i", j=PACK, i=4)
                 dst = w_grouped[g][:, e, :].rearrange("p (c i j) -> p c j i", j=PACK, i=4)
-                nc.vector.tensor_copy(out=dst, in_=src)
+                if e == 1 and g % 2 == 1:
+                    nc.scalar.copy(out=dst, in_=src)
+                else:
+                    nc.vector.tensor_copy(out=dst, in_=src)
 
         def quantise_w(g):
             wq_codes[g] = stage.tile([P, W_COLS], U32, name="wq_codes", align_bytes=64)
@@ -146,6 +145,29 @@ def tile_fgg_pa_k_kernel(tc, x, adjacency_matrix, W1, b1, Wr1_words, Wr1_scales,
                     stop=(g == PASSES - 1),
                 )
 
+        total = {}
+
+        def load_residual_weight(c):
+            chunk = slice(WR_CHUNK * c, WR_CHUNK * (c + 1))
+            nc.sync.dma_start(out=wr_codes[:, chunk, :].bitcast(I32), in_=wr_view[:, chunk, :].bitcast(I32))
+
+        def residual_passes(c):
+            if c == 0:
+                for t in range(NODE_TILES):
+                    total[t] = work_psum.tile([P, F_OUT], F32, tag="work", name="total%d" % t)
+            for g in range(WR_CHUNK * c, WR_CHUNK * (c + 1)):
+                for t in range(NODE_TILES):
+                    codes, scales = x_operand(g, t)
+                    nc.tensor.matmul_mx(
+                        out=total[t][:],
+                        lhsT=codes,
+                        lhsT_scale=scales,
+                        rhs=wr_codes[:, g, :].bitcast(FP8X4),
+                        rhs_scale=wr_scales[:, g, :],
+                        start=(g == 0),
+                        stop=False,
+                    )
+
         make_identity(nc, ident_bf16[:])
         make_identity(nc, ident_f32[:])
         nc.vector.memset(wr_scales[:].rearrange("p g n -> p (g n)").bitcast(I32), 0)
@@ -153,6 +175,11 @@ def tile_fgg_pa_k_kernel(tc, x, adjacency_matrix, W1, b1, Wr1_words, Wr1_scales,
         nc.sync.dma_start(out=adj_raw[:], in_=adj_view)
         for r in range(LEAD):
             load_x(r)
+        for row in range(4):
+            nc.sync.dma_start(
+                out=wr_scales[row:P:32, :, :].bitcast(I32),
+                in_=Wr1_scales[:, row:16:4, :].rearrange("g q n -> q g n").bitcast(I32),
+            )
 
         for e in range(EDGE_TYPES):
             for half in range(2):
@@ -185,6 +212,8 @@ def tile_fgg_pa_k_kernel(tc, x, adjacency_matrix, W1, b1, Wr1_words, Wr1_scales,
                 load_w(ROUND * r + i)
             if r + LEAD < ROUNDS:
                 load_x(r + LEAD)
+            else:
+                load_residual_weight(r + LEAD - ROUNDS)
             for i in range(ROUND):
                 regroup_w(ROUND * r + i)
                 if r + 1 < ROUNDS:
@@ -192,34 +221,16 @@ def tile_fgg_pa_k_kernel(tc, x, adjacency_matrix, W1, b1, Wr1_words, Wr1_scales,
                 quantise_w(ROUND * r + i)
             if r + LEAD < ROUNDS:
                 transpose_x(r + LEAD)
+            else:
+                residual_passes(r + LEAD - ROUNDS)
             for i in range(ROUND):
                 support_passes(ROUND * r + i)
 
-        for row in range(4):
-            nc.sync.dma_start(
-                out=wr_scales[row:P:32, :, :].bitcast(I32),
-                in_=Wr1_scales[:, row:16:4, :].rearrange("g q n -> q g n").bitcast(I32),
-            )
-        for c in range(4):
-            nc.sync.dma_start(
-                out=wr_codes[:, 4 * c : 4 * (c + 1), :].bitcast(I32),
-                in_=wr_view[:, 4 * c : 4 * (c + 1), :].bitcast(I32),
-            )
+        for c in range(LEAD, WR_CHUNKS):
+            load_residual_weight(c)
         nc.sync.dma_start(out=bias_bf16[:], in_=b1.partition_broadcast(P))
-
-        total = [work_psum.tile([P, F_OUT], F32, tag="work", name="total%d" % t) for t in range(NODE_TILES)]
-        for g in range(PASSES):
-            for t in range(NODE_TILES):
-                codes, scales = x_operand(g, t)
-                nc.tensor.matmul_mx(
-                    out=total[t][:],
-                    lhsT=codes,
-                    lhsT_scale=scales,
-                    rhs=wr_codes[:, g, :].bitcast(FP8X4),
-                    rhs_scale=wr_scales[:, g, :],
-                    start=(g == 0),
-                    stop=False,
-                )
+        for c in range(LEAD, WR_CHUNKS):
+            residual_passes(c)
         for t in range(NODE_TILES):
             if t % 2 == 0:
                 nc.vector.tensor_copy(out=sup_rows[:, t, :], in_=support[t][:])
@@ -229,12 +240,12 @@ def tile_fgg_pa_k_kernel(tc, x, adjacency_matrix, W1, b1, Wr1_words, Wr1_scales,
             out=sup_grouped[:].rearrange("p (c i) t -> p c t i", i=4),
             in_=sup_rows[:].rearrange("p t (c i) -> p c t i", i=4),
         )
-        nc.vector.tensor_copy(out=bias_f32[:], in_=bias_bf16[:])
         nc.vector.quantize_mx(
             out=supq_codes[:].bitcast(FP8X4),
             scales=supq_scales[:],
             in_=sup_grouped[:].rearrange("p c t -> p (c t)"),
         )
+        nc.vector.tensor_copy(out=bias_f32[:], in_=bias_bf16[:])
 
         for t in range(NODE_TILES):
             for e in range(EDGE_TYPES):

@@ -26,6 +26,7 @@ LEAD = 2
 W_COLS = EDGE_TYPES * F_OUT
 WR_CHUNK = 4
 WR_CHUNKS = PASSES // WR_CHUNK
+FILL = WR_CHUNK // ROUND
 
 FLOPS = 2 * NODES * FEATURES * (W_COLS + F_OUT) + 2 * EDGE_TYPES * NODES * NODES * F_OUT
 
@@ -82,24 +83,24 @@ def tile_fgg_pa_k_kernel(tc, x, adjacency_matrix, W1, b1, Wr1_words, Wr1_scales,
             for e in range(EDGE_TYPES):
                 nc.sync.dma_start(out=w_raw[g][:, e, :], in_=w1_view[e, g])
 
-        def transpose_x(r):
+        def transpose_x(r, i):
             words = x_raw[r][:].bitcast(F32)
-            x_grouped[r] = stage.tile([P, ROUND, NODES, PACK], BF16, name="x_grouped", align_bytes=64)
+            if i == 0:
+                x_grouped[r] = stage.tile([P, ROUND, NODES, PACK], BF16, name="x_grouped", align_bytes=64)
             grouped_words = x_grouped[r][:].bitcast(F32)
-            for i in range(ROUND):
-                for half in range(2):
-                    xt = work_psum.tile([P, 2, 2 * P], F32, tag="work")
-                    for u in range(2):
-                        for a in range(2):
-                            nc.tensor.transpose(
-                                xt[:, u, a * P : (a + 1) * P],
-                                words[:, 2 * half + a, 256 * i + u : 256 * (i + 1) : 2],
-                                ident_f32[:],
-                            )
-                    nc.scalar.copy(
-                        out=grouped_words[:, i, 2 * P * half : 2 * P * (half + 1), :],
-                        in_=xt[:].rearrange("p u n -> p n u"),
-                    )
+            for half in range(2):
+                xt = work_psum.tile([P, 2, 2 * P], F32, tag="work")
+                for u in range(2):
+                    for a in range(2):
+                        nc.tensor.transpose(
+                            xt[:, u, a * P : (a + 1) * P],
+                            words[:, 2 * half + a, 256 * i + u : 256 * (i + 1) : 2],
+                            ident_f32[:],
+                        )
+                nc.scalar.copy(
+                    out=grouped_words[:, i, 2 * P * half : 2 * P * (half + 1), :],
+                    in_=xt[:].rearrange("p u n -> p n u"),
+                )
 
         def quantise_x(r, i):
             g = ROUND * r + i
@@ -151,11 +152,11 @@ def tile_fgg_pa_k_kernel(tc, x, adjacency_matrix, W1, b1, Wr1_words, Wr1_scales,
             chunk = slice(WR_CHUNK * c, WR_CHUNK * (c + 1))
             nc.sync.dma_start(out=wr_codes[:, chunk, :].bitcast(I32), in_=wr_view[:, chunk, :].bitcast(I32))
 
-        def residual_passes(c):
-            if c == 0:
+        def residual_passes(first, count):
+            if first == 0:
                 for t in range(NODE_TILES):
                     total[t] = work_psum.tile([P, F_OUT], F32, tag="work", name="total%d" % t)
-            for g in range(WR_CHUNK * c, WR_CHUNK * (c + 1)):
+            for g in range(first, first + count):
                 for t in range(NODE_TILES):
                     codes, scales = x_operand(g, t)
                     nc.tensor.matmul_mx(
@@ -204,7 +205,8 @@ def tile_fgg_pa_k_kernel(tc, x, adjacency_matrix, W1, b1, Wr1_words, Wr1_scales,
         )
 
         for r in range(LEAD):
-            transpose_x(r)
+            for i in range(ROUND):
+                transpose_x(r, i)
         for i in range(ROUND):
             quantise_x(0, i)
         for r in range(ROUNDS):
@@ -219,18 +221,17 @@ def tile_fgg_pa_k_kernel(tc, x, adjacency_matrix, W1, b1, Wr1_words, Wr1_scales,
                 if r + 1 < ROUNDS:
                     quantise_x(r + 1, i)
                 quantise_w(ROUND * r + i)
-            if r + LEAD < ROUNDS:
-                transpose_x(r + LEAD)
-            else:
-                residual_passes(r + LEAD - ROUNDS)
             for i in range(ROUND):
+                if r + LEAD < ROUNDS:
+                    transpose_x(r + LEAD, i)
+                else:
+                    residual_passes(WR_CHUNK * (r + LEAD - ROUNDS) + FILL * i, FILL)
                 support_passes(ROUND * r + i)
 
         for c in range(LEAD, WR_CHUNKS):
             load_residual_weight(c)
         nc.sync.dma_start(out=bias_bf16[:], in_=b1.partition_broadcast(P))
-        for c in range(LEAD, WR_CHUNKS):
-            residual_passes(c)
+        residual_passes(WR_CHUNK * LEAD, PASSES - WR_CHUNK * LEAD)
         for t in range(NODE_TILES):
             if t % 2 == 0:
                 nc.vector.tensor_copy(out=sup_rows[:, t, :], in_=support[t][:])

@@ -22,11 +22,9 @@ NODE_TILES = NODES // P
 PASSES = FEATURES // K_PASS
 ROUND = 2
 ROUNDS = PASSES // ROUND
-LEAD = 2
 W_COLS = EDGE_TYPES * F_OUT
 WR_CHUNK = 4
-WR_CHUNKS = PASSES // WR_CHUNK
-FILL = WR_CHUNK // ROUND
+QUADS = F_OUT // 4
 
 FLOPS = 2 * NODES * FEATURES * (W_COLS + F_OUT) + 2 * EDGE_TYPES * NODES * NODES * F_OUT
 
@@ -36,32 +34,31 @@ def tile_fgg_pa_k_kernel(tc, x, adjacency_matrix, W1, b1, Wr1_words, Wr1_scales,
     with ExitStack() as ctx:
         ctx.enter_context(tc.manual_schedule())
         keep = ctx.enter_context(tc.tile_pool(name="keep", bufs=1))
-        raw = ctx.enter_context(tc.tile_pool(name="raw", bufs=4))
+        x_pool = ctx.enter_context(tc.tile_pool(name="x_pool", bufs=2))
+        w_pool = ctx.enter_context(tc.tile_pool(name="w_pool", bufs=8))
         stage = ctx.enter_context(tc.tile_pool(name="stage", bufs=4))
         sup_psum = ctx.enter_context(tc.psum_pool(name="sup_psum", bufs=1))
         work_psum = ctx.enter_context(tc.psum_pool(name="work_psum", bufs=4))
 
-        x_view = x.rearrange("(t p) k -> p t k", p=P)
-        adj_view = adjacency_matrix.rearrange("e (t p) m -> p (e t) m", p=P)
-        w1_view = W1.rearrange("e (g p j) w -> e g p (j w)", p=P, j=PACK)
+        x_view = x.rearrange("(u p f) k -> u p f k", u=2, f=2)
+        adj_view = adjacency_matrix.rearrange("e (u p f) m -> e u p (f m)", u=2, f=2)
+        w1_view = W1.rearrange("e (g p j) w -> g p e (j w)", p=P, j=PACK)
         wr_view = Wr1_words.rearrange("g p n t -> p g (n t)")
-        out_view = out.rearrange("(t p) f -> t p f", p=P)
+        out_view = out.rearrange("(u p f) c -> u f p c", u=2, f=2)
 
         ident_f32 = keep.tile([P, P], F32)
-        ident_bf16 = keep.tile([P, P], BF16)
+        ones = keep.tile([P, P], BF16)
         xq_codes = keep.tile([P, PASSES * NODES], U32, align_bytes=64)
         xq_scales = keep.tile([P, PASSES * NODES], U8, align_bytes=64)
         wr_codes = keep.tile([P, PASSES, F_OUT], U32, align_bytes=64)
         wr_scales = keep.tile([P, PASSES, F_OUT], U8, align_bytes=64)
-        adj_raw = keep.tile([P, EDGE_TYPES * NODE_TILES, NODES], BF16)
-        adj_grouped = keep.tile([P, EDGE_TYPES, NODES, PACK], BF16, align_bytes=64)
         adjq_codes = keep.tile([P, EDGE_TYPES * NODES], U32, align_bytes=64)
         adjq_scales = keep.tile([P, EDGE_TYPES * NODES], U8, align_bytes=64)
         sup_rows = keep.tile([P, NODE_TILES, W_COLS], BF16)
         sup_grouped = keep.tile([P, W_COLS, PACK], BF16, align_bytes=64)
         supq_codes = keep.tile([P, W_COLS], U32, align_bytes=64)
         supq_scales = keep.tile([P, W_COLS], U8, align_bytes=64)
-        bias_bf16 = keep.tile([P, F_OUT], BF16)
+        bias_row = keep.tile([P, F_OUT], BF16)
         bias_f32 = keep.tile([P, F_OUT], F32)
         result = keep.tile([P, NODE_TILES, F_OUT], F32)
 
@@ -74,29 +71,62 @@ def tile_fgg_pa_k_kernel(tc, x, adjacency_matrix, W1, b1, Wr1_words, Wr1_scales,
         wq_codes = {}
         wq_scales = {}
 
-        def load_x(r):
-            x_raw[r] = raw.tile([P, NODE_TILES, ROUND * K_PASS], BF16, name="x_raw")
-            nc.sync.dma_start(out=x_raw[r][:], in_=x_view[:, :, r * ROUND * K_PASS : (r + 1) * ROUND * K_PASS])
+        x_first = {}
+
+        def load_first_x(i):
+            x_first[i] = x_pool.tile([P, NODE_TILES, K_PASS], BF16, name="x_first", tag="x_first", bufs=ROUND)
+            there = slice(i * K_PASS, (i + 1) * K_PASS)
+            for u in range(2):
+                nc.sync.dma_start(out=x_first[i][:, 2 * u : 2 * u + 2, :], in_=x_view[u][:, :, there])
+
+        def load_x(r, count):
+            chunk = x_pool.tile([P, NODE_TILES, count * ROUND * K_PASS], BF16, name="x_raw%d" % count, tag="x_raw%d" % count, bufs=4)
+            there = slice(ROUND * r * K_PASS, ROUND * (r + count) * K_PASS)
+            for u in range(2):
+                nc.sync.dma_start(out=chunk[:, 2 * u : 2 * u + 2, :], in_=x_view[u][:, :, there])
+            for n in range(count):
+                x_raw[r + n] = chunk[:, :, n * ROUND * K_PASS : (n + 1) * ROUND * K_PASS]
 
         def load_w(g):
-            w_raw[g] = raw.tile([P, EDGE_TYPES, PACK * F_OUT], BF16, name="w_raw")
+            w_raw[g] = w_pool.tile([P, EDGE_TYPES, PACK * F_OUT], BF16, name="w_raw")
+            nc.sync.dma_start(out=w_raw[g][:], in_=w1_view[g])
+
+        def load_wr(c):
+            here = slice(WR_CHUNK * c, WR_CHUNK * (c + 1))
+            nc.sync.dma_start(out=wr_codes[:, here, :].bitcast(I32), in_=wr_view[:, here, :].bitcast(I32))
+
+        def load_wr_scales():
+            for row in range(4):
+                nc.sync.dma_start(
+                    out=wr_scales[row:P:32, :, :].bitcast(I32),
+                    in_=Wr1_scales[:, row:16:4, :].rearrange("g q n -> q g n").bitcast(I32),
+                )
+
+        adj_raw = {}
+
+        def load_adj():
+            adj_raw[0] = x_pool.tile([P, EDGE_TYPES * NODE_TILES, NODES], BF16, name="adj_raw", tag="x_raw1", bufs=4)
             for e in range(EDGE_TYPES):
-                nc.sync.dma_start(out=w_raw[g][:, e, :], in_=w1_view[e, g])
+                for u in range(2):
+                    first = e * NODE_TILES + 2 * u
+                    nc.sync.dma_start(
+                        out=adj_raw[0][:, first : first + 2, :].rearrange("p f m -> p (f m)"),
+                        in_=adj_view[e, u],
+                    )
 
         def transpose_x(r, i):
-            words = x_raw[r][:].bitcast(F32)
             if i == 0:
-                x_grouped[r] = stage.tile([P, ROUND, NODES, PACK], BF16, name="x_grouped", align_bytes=64)
+                x_grouped[r] = stage.tile([P, ROUND, NODES, PACK], BF16, name="x_grouped", tag="grouped", bufs=3, align_bytes=64)
             grouped_words = x_grouped[r][:].bitcast(F32)
             for half in range(2):
                 xt = work_psum.tile([P, 2, 2 * P], F32, tag="work")
                 for u in range(2):
                     for a in range(2):
-                        nc.tensor.transpose(
-                            xt[:, u, a * P : (a + 1) * P],
-                            words[:, 2 * half + a, 256 * i + u : 256 * (i + 1) : 2],
-                            ident_f32[:],
-                        )
+                        if r == 0:
+                            words = x_first[i][:].bitcast(F32)[:, 2 * half + a, u:256:2]
+                        else:
+                            words = x_raw[r].bitcast(F32)[:, 2 * half + a, 256 * i + u : 256 * (i + 1) : 2]
+                        nc.tensor.transpose(xt[:, u, a * P : (a + 1) * P], words, ident_f32[:])
                 nc.scalar.copy(
                     out=grouped_words[:, i, 2 * P * half : 2 * P * (half + 1), :],
                     in_=xt[:].rearrange("p u n -> p n u"),
@@ -110,15 +140,19 @@ def tile_fgg_pa_k_kernel(tc, x, adjacency_matrix, W1, b1, Wr1_words, Wr1_scales,
                 in_=x_grouped[r][:, i].rearrange("p n t -> p (n t)"),
             )
 
-        def regroup_w(g):
-            w_grouped[g] = stage.tile([P, EDGE_TYPES, F_OUT * PACK], BF16, name="w_grouped", align_bytes=64)
-            for e in range(EDGE_TYPES):
-                src = w_raw[g][:, e, :].rearrange("p (j c i) -> p c j i", j=PACK, i=4)
-                dst = w_grouped[g][:, e, :].rearrange("p (c i j) -> p c j i", j=PACK, i=4)
-                if e == 1 and g % 2 == 1:
-                    nc.scalar.copy(out=dst, in_=src)
-                else:
-                    nc.vector.tensor_copy(out=dst, in_=src)
+        def x_operand(g, t):
+            cols = slice(g * NODES + t * P, g * NODES + (t + 1) * P)
+            return xq_codes[:, cols].bitcast(FP8X4), xq_scales[:, cols]
+
+        def regroup_w(g, e, engine):
+            if g not in w_grouped:
+                w_grouped[g] = stage.tile([P, EDGE_TYPES, F_OUT * PACK], BF16, name="w_grouped", align_bytes=64)
+            src = w_raw[g][:, e, :].rearrange("p (j c i) -> p c j i", j=PACK, i=4)
+            dst = w_grouped[g][:, e, :].rearrange("p (c i j) -> p c j i", j=PACK, i=4)
+            if engine == "scalar":
+                nc.scalar.copy(out=dst, in_=src)
+            else:
+                nc.vector.tensor_copy(out=dst, in_=src)
 
         def quantise_w(g):
             wq_codes[g] = stage.tile([P, W_COLS], U32, name="wq_codes", align_bytes=64)
@@ -128,10 +162,6 @@ def tile_fgg_pa_k_kernel(tc, x, adjacency_matrix, W1, b1, Wr1_words, Wr1_scales,
                 scales=wq_scales[g][:],
                 in_=w_grouped[g][:].rearrange("p e n -> p (e n)"),
             )
-
-        def x_operand(g, t):
-            cols = slice(g * NODES + t * P, g * NODES + (t + 1) * P)
-            return xq_codes[:, cols].bitcast(FP8X4), xq_scales[:, cols]
 
         def support_passes(g):
             for t in range(NODE_TILES):
@@ -148,90 +178,103 @@ def tile_fgg_pa_k_kernel(tc, x, adjacency_matrix, W1, b1, Wr1_words, Wr1_scales,
 
         total = {}
 
-        def load_residual_weight(c):
-            chunk = slice(WR_CHUNK * c, WR_CHUNK * (c + 1))
-            nc.sync.dma_start(out=wr_codes[:, chunk, :].bitcast(I32), in_=wr_view[:, chunk, :].bitcast(I32))
-
-        def residual_passes(first, count):
-            if first == 0:
-                for t in range(NODE_TILES):
+        def residual_passes(g):
+            for t in range(NODE_TILES):
+                if g == 0:
                     total[t] = work_psum.tile([P, F_OUT], F32, tag="work", name="total%d" % t)
-            for g in range(first, first + count):
-                for t in range(NODE_TILES):
-                    codes, scales = x_operand(g, t)
-                    nc.tensor.matmul_mx(
-                        out=total[t][:],
-                        lhsT=codes,
-                        lhsT_scale=scales,
-                        rhs=wr_codes[:, g, :].bitcast(FP8X4),
-                        rhs_scale=wr_scales[:, g, :],
-                        start=(g == 0),
-                        stop=False,
+                codes, scales = x_operand(g, t)
+                nc.tensor.matmul_mx(
+                    out=total[t][:],
+                    lhsT=codes,
+                    lhsT_scale=scales,
+                    rhs=wr_codes[:, g, :].bitcast(FP8X4),
+                    rhs_scale=wr_scales[:, g, :],
+                    start=(g == 0),
+                    stop=False,
+                )
+
+        adj_grouped = {}
+
+        def transpose_adj():
+            adj_grouped[0] = stage.tile([P, EDGE_TYPES, NODES, PACK], BF16, name="adj_grouped", tag="grouped", bufs=3, align_bytes=64)
+            words = adj_raw[0][:].bitcast(F32)
+            for e in range(EDGE_TYPES):
+                for half in range(2):
+                    at = work_psum.tile([P, 2, 2 * P], F32, tag="work")
+                    for u in range(2):
+                        for a in range(2):
+                            nc.tensor.transpose(
+                                at[:, u, a * P : (a + 1) * P],
+                                words[:, e * NODE_TILES + 2 * half + a, P * u : P * (u + 1)],
+                                ident_f32[:],
+                            )
+                    nc.scalar.copy(
+                        out=adj_grouped[0][:].bitcast(F32)[:, e, 2 * P * half : 2 * P * (half + 1), :],
+                        in_=at[:].rearrange("p u n -> p n u"),
                     )
 
-        make_identity(nc, ident_bf16[:])
-        make_identity(nc, ident_f32[:])
-        nc.vector.memset(wr_scales[:].rearrange("p g n -> p (g n)").bitcast(I32), 0)
-
-        nc.sync.dma_start(out=adj_raw[:], in_=adj_view)
-        for r in range(LEAD):
-            load_x(r)
-        for row in range(4):
-            nc.sync.dma_start(
-                out=wr_scales[row:P:32, :, :].bitcast(I32),
-                in_=Wr1_scales[:, row:16:4, :].rearrange("g q n -> q g n").bitcast(I32),
+        def quantise_adj():
+            nc.vector.quantize_mx(
+                out=adjq_codes[:].bitcast(FP8X4),
+                scales=adjq_scales[:],
+                in_=adj_grouped[0][:].rearrange("p e n t -> p (e n t)"),
             )
 
-        for e in range(EDGE_TYPES):
-            for half in range(2):
-                at = work_psum.tile([P, 2, PACK, P], BF16, tag="work")
-                for a in range(2):
-                    for t in range(PACK):
-                        nc.tensor.transpose(
-                            at[:, a, t, :],
-                            adj_raw[:, e * NODE_TILES + 2 * half + a, t * P : (t + 1) * P],
-                            ident_bf16[:],
-                        )
-                dst = adj_grouped[:, e, 2 * P * half : 2 * P * (half + 1), :].rearrange("p (a r) t -> p a r t", a=2)
-                src = at[:].rearrange("p a t r -> p a r t")
-                if half == 0:
-                    nc.vector.tensor_copy(out=dst, in_=src)
-                else:
-                    nc.scalar.copy(out=dst, in_=src)
-        nc.vector.quantize_mx(
-            out=adjq_codes[:].bitcast(FP8X4),
-            scales=adjq_scales[:],
-            in_=adj_grouped[:].rearrange("p e n t -> p (e n t)"),
-        )
+        load_first_x(0)
+        load_w(0)
+        load_first_x(1)
+        load_w(1)
+        make_identity(nc, ident_f32[:])
+        nc.vector.memset(wr_scales[:].rearrange("p g n -> p (g n)").bitcast(I32), 0)
+        nc.vector.memset(bias_row[:], 0.0)
+        nc.vector.memset(ones[:], 1.0)
+        load_x(1, 1)
+        load_w(2)
+        load_w(3)
+        nc.sync.dma_start(out=bias_row[0:1, :], in_=b1.unsqueeze(0))
+        for r in (2, 3):
+            load_x(r, 1)
+            load_w(ROUND * r)
+            load_w(ROUND * r + 1)
 
-        for r in range(LEAD):
+        def prepare(r):
             for i in range(ROUND):
-                transpose_x(r, i)
-        for i in range(ROUND):
-            quantise_x(0, i)
+                g = ROUND * r + i
+                regroup_w(g, 0, "vector")
+                regroup_w(g, 1, "vector" if g % 4 == 0 else "scalar")
+                quantise_x(r, i)
+                quantise_w(g)
+
+        def passes(r):
+            for g in range(ROUND * r, ROUND * (r + 1)):
+                support_passes(g)
+
         for r in range(ROUNDS):
             for i in range(ROUND):
-                load_w(ROUND * r + i)
-            if r + LEAD < ROUNDS:
-                load_x(r + LEAD)
-            else:
-                load_residual_weight(r + LEAD - ROUNDS)
-            for i in range(ROUND):
-                regroup_w(ROUND * r + i)
-                if r + 1 < ROUNDS:
-                    quantise_x(r + 1, i)
-                quantise_w(ROUND * r + i)
-            for i in range(ROUND):
-                if r + LEAD < ROUNDS:
-                    transpose_x(r + LEAD, i)
-                else:
-                    residual_passes(WR_CHUNK * (r + LEAD - ROUNDS) + FILL * i, FILL)
-                support_passes(ROUND * r + i)
-
-        for c in range(LEAD, WR_CHUNKS):
-            load_residual_weight(c)
-        nc.sync.dma_start(out=bias_bf16[:], in_=b1.partition_broadcast(P))
-        residual_passes(WR_CHUNK * LEAD, PASSES - WR_CHUNK * LEAD)
+                transpose_x(r, i)
+            if r >= 2:
+                passes(r - 1)
+            prepare(r)
+            if r == 0:
+                passes(0)
+            if r + 4 < ROUNDS:
+                load_x(r + 4, 1)
+                load_w(ROUND * (r + 4))
+                load_w(ROUND * (r + 4) + 1)
+            if r == 4:
+                load_adj()
+                load_wr_scales()
+                for c in range(PASSES // WR_CHUNK):
+                    load_wr(c)
+            if r == ROUNDS - 1:
+                bias_sum = work_psum.tile([P, F_OUT], F32, tag="work")
+                nc.tensor.matmul(bias_sum[:], lhsT=ones[:], rhs=bias_row[:], start=True, stop=True)
+                nc.scalar.copy(out=bias_f32[:], in_=bias_sum[:])
+                transpose_adj()
+                quantise_adj()
+        passes(ROUNDS - 1)
+        for g in range(PASSES):
+            residual_passes(g)
         for t in range(NODE_TILES):
             if t % 2 == 0:
                 nc.vector.tensor_copy(out=sup_rows[:, t, :], in_=support[t][:])
@@ -246,7 +289,6 @@ def tile_fgg_pa_k_kernel(tc, x, adjacency_matrix, W1, b1, Wr1_words, Wr1_scales,
             scales=supq_scales[:],
             in_=sup_grouped[:].rearrange("p c t -> p (c t)"),
         )
-        nc.vector.tensor_copy(out=bias_f32[:], in_=bias_bf16[:])
 
         for t in range(NODE_TILES):
             for e in range(EDGE_TYPES):
@@ -262,4 +304,4 @@ def tile_fgg_pa_k_kernel(tc, x, adjacency_matrix, W1, b1, Wr1_words, Wr1_scales,
                     stop=(e == EDGE_TYPES - 1),
                 )
             nc.vector.tensor_tensor(out=result[:, t, :], in0=total[t][:], in1=bias_f32[:], op=ADD)
-            nc.sync.dma_start(out=out_view[t], in_=result[:, t, :])
+            nc.sync.dma_start(out=out_view[t // 2, t % 2], in_=result[:, t, :])

@@ -24,7 +24,7 @@ ROUND = 2
 ROUNDS = PASSES // ROUND
 W_COLS = EDGE_TYPES * F_OUT
 WR_CHUNK = 4
-QUADS = F_OUT // 4
+LEAD = 2
 
 FLOPS = 2 * NODES * FEATURES * (W_COLS + F_OUT) + 2 * EDGE_TYPES * NODES * NODES * F_OUT
 
@@ -116,7 +116,7 @@ def tile_fgg_pa_k_kernel(tc, x, adjacency_matrix, W1, b1, Wr1_words, Wr1_scales,
 
         def transpose_x(r, i):
             if i == 0:
-                x_grouped[r] = stage.tile([P, ROUND, NODES, PACK], BF16, name="x_grouped", tag="grouped", bufs=3, align_bytes=64)
+                x_grouped[r] = stage.tile([P, ROUND, NODES, PACK], BF16, name="x_grouped", tag="grouped", bufs=4, align_bytes=64)
             grouped_words = x_grouped[r][:].bitcast(F32)
             for half in range(2):
                 xt = work_psum.tile([P, 2, 2 * P], F32, tag="work")
@@ -196,7 +196,7 @@ def tile_fgg_pa_k_kernel(tc, x, adjacency_matrix, W1, b1, Wr1_words, Wr1_scales,
         adj_grouped = {}
 
         def transpose_adj():
-            adj_grouped[0] = stage.tile([P, EDGE_TYPES, NODES, PACK], BF16, name="adj_grouped", tag="grouped", bufs=3, align_bytes=64)
+            adj_grouped[0] = stage.tile([P, EDGE_TYPES, NODES, PACK], BF16, name="adj_grouped", tag="grouped", bufs=4, align_bytes=64)
             words = adj_raw[0][:].bitcast(F32)
             for e in range(EDGE_TYPES):
                 for half in range(2):
@@ -228,51 +228,44 @@ def tile_fgg_pa_k_kernel(tc, x, adjacency_matrix, W1, b1, Wr1_words, Wr1_scales,
         nc.vector.memset(wr_scales[:].rearrange("p g n -> p (g n)").bitcast(I32), 0)
         nc.vector.memset(bias_row[:], 0.0)
         nc.vector.memset(ones[:], 1.0)
-        load_x(1, 1)
-        load_w(2)
-        load_w(3)
         nc.sync.dma_start(out=bias_row[0:1, :], in_=b1.unsqueeze(0))
-        for r in (2, 3):
+        for r in (1, 2, 3):
             load_x(r, 1)
             load_w(ROUND * r)
             load_w(ROUND * r + 1)
 
-        def prepare(r):
-            for i in range(ROUND):
-                g = ROUND * r + i
-                regroup_w(g, 0, "vector")
-                regroup_w(g, 1, "vector" if g % 4 == 0 else "scalar")
-                quantise_x(r, i)
-                quantise_w(g)
+        def prepare(g):
+            regroup_w(g, 0, "vector")
+            regroup_w(g, 1, "vector" if g % 4 == 0 else "scalar")
+            quantise_x(g // ROUND, g % ROUND)
+            quantise_w(g)
 
-        def passes(r):
-            for g in range(ROUND * r, ROUND * (r + 1)):
-                support_passes(g)
-
-        for r in range(ROUNDS):
-            for i in range(ROUND):
-                transpose_x(r, i)
-            if r >= 2:
-                passes(r - 1)
-            prepare(r)
-            if r == 0:
-                passes(0)
-            if r + 4 < ROUNDS:
-                load_x(r + 4, 1)
-                load_w(ROUND * (r + 4))
-                load_w(ROUND * (r + 4) + 1)
-            if r == 4:
+        for g in range(LEAD):
+            transpose_x(g // ROUND, g % ROUND)
+            prepare(g)
+        for g in range(PASSES):
+            if g + LEAD < PASSES:
+                transpose_x((g + LEAD) // ROUND, (g + LEAD) % ROUND)
+            support_passes(g)
+            if g + LEAD < PASSES:
+                prepare(g + LEAD)
+            if g == 0:
+                bias_sum = work_psum.tile([P, F_OUT], F32, tag="work")
+                nc.tensor.matmul(bias_sum[:], lhsT=ones[:], rhs=bias_row[:], start=True, stop=True)
+                nc.scalar.copy(out=bias_f32[:], in_=bias_sum[:])
+            if g % ROUND == 1 and g // ROUND + 4 < ROUNDS:
+                r = g // ROUND + 4
+                load_x(r, 1)
+                load_w(ROUND * r)
+                load_w(ROUND * r + 1)
+            if g == 9:
                 load_adj()
                 load_wr_scales()
                 for c in range(PASSES // WR_CHUNK):
                     load_wr(c)
-            if r == ROUNDS - 1:
-                bias_sum = work_psum.tile([P, F_OUT], F32, tag="work")
-                nc.tensor.matmul(bias_sum[:], lhsT=ones[:], rhs=bias_row[:], start=True, stop=True)
-                nc.scalar.copy(out=bias_f32[:], in_=bias_sum[:])
+            if g == PASSES - 2:
                 transpose_adj()
                 quantise_adj()
-        passes(ROUNDS - 1)
         for g in range(PASSES):
             residual_passes(g)
         for t in range(NODE_TILES):

@@ -23,7 +23,6 @@ PASSES = FEATURES // K_PASS
 ROUND = 2
 ROUNDS = PASSES // ROUND
 W_COLS = EDGE_TYPES * F_OUT
-WR_CHUNK = 4
 LEAD = 2
 
 FLOPS = 2 * NODES * FEATURES * (W_COLS + F_OUT) + 2 * EDGE_TYPES * NODES * NODES * F_OUT
@@ -91,8 +90,8 @@ def tile_fgg_pa_k_kernel(tc, x, adjacency_matrix, W1, b1, Wr1_words, Wr1_scales,
             w_raw[g] = w_pool.tile([P, EDGE_TYPES, PACK * F_OUT], BF16, name="w_raw")
             nc.sync.dma_start(out=w_raw[g][:], in_=w1_view[g])
 
-        def load_wr(c):
-            here = slice(WR_CHUNK * c, WR_CHUNK * (c + 1))
+        def load_wr(first, count):
+            here = slice(first, first + count)
             nc.sync.dma_start(out=wr_codes[:, here, :].bitcast(I32), in_=wr_view[:, here, :].bitcast(I32))
 
         def load_wr_scales():
@@ -114,30 +113,41 @@ def tile_fgg_pa_k_kernel(tc, x, adjacency_matrix, W1, b1, Wr1_words, Wr1_scales,
                         in_=adj_view[e, u],
                     )
 
-        def transpose_x(r, i):
-            if i == 0:
-                x_grouped[r] = stage.tile([P, ROUND, NODES, PACK], BF16, name="x_grouped", tag="grouped", bufs=4, align_bytes=64)
-            grouped_words = x_grouped[r][:].bitcast(F32)
+        x_sorted = {}
+
+        def sort_x(g):
+            r, i = g // ROUND, g % ROUND
+            x_sorted[g] = stage.tile([P, NODE_TILES, K_PASS], BF16, name="x_sorted", tag="x_sorted", bufs=3)
+            nc.vector.tensor_copy(
+                out=x_sorted[g][:].bitcast(F32).rearrange("p t (u w) -> p t u w", u=2),
+                in_=x_raw[r].bitcast(F32)[:, :, 256 * i : 256 * (i + 1)].rearrange("p t (w u) -> p t u w", u=2),
+            )
+
+        def transpose_x(g):
+            r, i = g // ROUND, g % ROUND
+            x_grouped[g] = stage.tile([P, NODES, PACK], BF16, name="x_grouped", tag="x_grouped", bufs=4, align_bytes=64)
             for half in range(2):
                 xt = work_psum.tile([P, 2, 2 * P], F32, tag="work")
                 for u in range(2):
                     for a in range(2):
-                        if r == 0:
-                            words = x_first[i][:].bitcast(F32)[:, 2 * half + a, u:256:2]
+                        t = 2 * half + a
+                        if g in x_sorted:
+                            words = x_sorted[g][:].bitcast(F32)[:, t, P * u : P * (u + 1)]
+                        elif r == 0:
+                            words = x_first[i][:].bitcast(F32)[:, t, u:256:2]
                         else:
-                            words = x_raw[r].bitcast(F32)[:, 2 * half + a, 256 * i + u : 256 * (i + 1) : 2]
+                            words = x_raw[r].bitcast(F32)[:, t, 256 * i + u : 256 * (i + 1) : 2]
                         nc.tensor.transpose(xt[:, u, a * P : (a + 1) * P], words, ident_f32[:])
                 nc.scalar.copy(
-                    out=grouped_words[:, i, 2 * P * half : 2 * P * (half + 1), :],
+                    out=x_grouped[g][:].bitcast(F32)[:, 2 * P * half : 2 * P * (half + 1), :],
                     in_=xt[:].rearrange("p u n -> p n u"),
                 )
 
-        def quantise_x(r, i):
-            g = ROUND * r + i
+        def quantise_x(g):
             nc.vector.quantize_mx(
                 out=xq_codes[:, g * NODES : (g + 1) * NODES].bitcast(FP8X4),
                 scales=xq_scales[:, g * NODES : (g + 1) * NODES],
-                in_=x_grouped[r][:, i].rearrange("p n t -> p (n t)"),
+                in_=x_grouped[g][:].rearrange("p n t -> p (n t)"),
             )
 
         def x_operand(g, t):
@@ -178,46 +188,79 @@ def tile_fgg_pa_k_kernel(tc, x, adjacency_matrix, W1, b1, Wr1_words, Wr1_scales,
 
         total = {}
 
-        def residual_passes(g):
-            for t in range(NODE_TILES):
-                if g == 0:
-                    total[t] = work_psum.tile([P, F_OUT], F32, tag="work", name="total%d" % t)
-                codes, scales = x_operand(g, t)
-                nc.tensor.matmul_mx(
-                    out=total[t][:],
-                    lhsT=codes,
-                    lhsT_scale=scales,
-                    rhs=wr_codes[:, g, :].bitcast(FP8X4),
-                    rhs_scale=wr_scales[:, g, :],
-                    start=(g == 0),
-                    stop=False,
-                )
+        def residual_pass(g, t):
+            if g == 0:
+                total[t] = work_psum.tile([P, F_OUT], F32, tag="work", name="total%d" % t)
+            codes, scales = x_operand(g, t)
+            nc.tensor.matmul_mx(
+                out=total[t][:],
+                lhsT=codes,
+                lhsT_scale=scales,
+                rhs=wr_codes[:, g, :].bitcast(FP8X4),
+                rhs_scale=wr_scales[:, g, :],
+                start=(g == 0),
+                stop=(g == PASSES - 1),
+            )
+
+        def aggregate(e, t):
+            n_cols = slice(e * NODES + t * P, e * NODES + (t + 1) * P)
+            f_cols = slice(e * F_OUT, (e + 1) * F_OUT)
+            nc.tensor.matmul_mx(
+                out=total[t][:],
+                lhsT=adjq_codes[:, n_cols].bitcast(FP8X4),
+                lhsT_scale=adjq_scales[:, n_cols],
+                rhs=supq_codes[:, f_cols].bitcast(FP8X4),
+                rhs_scale=supq_scales[:, f_cols],
+                start=False,
+                stop=False,
+            )
 
         adj_grouped = {}
 
-        def transpose_adj():
-            adj_grouped[0] = stage.tile([P, EDGE_TYPES, NODES, PACK], BF16, name="adj_grouped", tag="grouped", bufs=4, align_bytes=64)
+        def transpose_adj(e):
+            adj_grouped[e] = stage.tile([P, NODES, PACK], BF16, name="adj_grouped", tag="x_grouped", bufs=4, align_bytes=64)
             words = adj_raw[0][:].bitcast(F32)
-            for e in range(EDGE_TYPES):
-                for half in range(2):
-                    at = work_psum.tile([P, 2, 2 * P], F32, tag="work")
-                    for u in range(2):
-                        for a in range(2):
-                            nc.tensor.transpose(
-                                at[:, u, a * P : (a + 1) * P],
-                                words[:, e * NODE_TILES + 2 * half + a, P * u : P * (u + 1)],
-                                ident_f32[:],
-                            )
-                    nc.scalar.copy(
-                        out=adj_grouped[0][:].bitcast(F32)[:, e, 2 * P * half : 2 * P * (half + 1), :],
-                        in_=at[:].rearrange("p u n -> p n u"),
-                    )
+            for half in range(2):
+                at = work_psum.tile([P, 2, 2 * P], F32, tag="work")
+                for u in range(2):
+                    for a in range(2):
+                        nc.tensor.transpose(
+                            at[:, u, a * P : (a + 1) * P],
+                            words[:, e * NODE_TILES + 2 * half + a, P * u : P * (u + 1)],
+                            ident_f32[:],
+                        )
+                nc.scalar.copy(
+                    out=adj_grouped[e][:].bitcast(F32)[:, 2 * P * half : 2 * P * (half + 1), :],
+                    in_=at[:].rearrange("p u n -> p n u"),
+                )
 
-        def quantise_adj():
+        def quantise_adj(e):
+            nodes = slice(e * NODES, (e + 1) * NODES)
             nc.vector.quantize_mx(
-                out=adjq_codes[:].bitcast(FP8X4),
-                scales=adjq_scales[:],
-                in_=adj_grouped[0][:].rearrange("p e n t -> p (e n t)"),
+                out=adjq_codes[:, nodes].bitcast(FP8X4),
+                scales=adjq_scales[:, nodes],
+                in_=adj_grouped[e][:].rearrange("p n t -> p (n t)"),
+            )
+
+        def support_rows(t, engine):
+            if engine == "scalar":
+                nc.scalar.copy(out=sup_rows[:, t, :], in_=support[t][:])
+            else:
+                nc.vector.tensor_copy(out=sup_rows[:, t, :], in_=support[t][:])
+
+        def regroup_support(e):
+            f_cols = slice(e * F_OUT, (e + 1) * F_OUT)
+            nc.vector.tensor_copy(
+                out=sup_grouped[:, f_cols, :].rearrange("p (c i) t -> p c t i", i=4),
+                in_=sup_rows[:, :, f_cols].rearrange("p t (c i) -> p c t i", i=4),
+            )
+
+        def quantise_support(e):
+            f_cols = slice(e * F_OUT, (e + 1) * F_OUT)
+            nc.vector.quantize_mx(
+                out=supq_codes[:, f_cols].bitcast(FP8X4),
+                scales=supq_scales[:, f_cols],
+                in_=sup_grouped[:, f_cols, :].rearrange("p c t -> p (c t)"),
             )
 
         load_first_x(0)
@@ -235,20 +278,29 @@ def tile_fgg_pa_k_kernel(tc, x, adjacency_matrix, W1, b1, Wr1_words, Wr1_scales,
             load_w(ROUND * r + 1)
 
         def prepare(g):
-            regroup_w(g, 0, "vector")
-            regroup_w(g, 1, "vector" if g % 4 == 0 else "scalar")
-            quantise_x(g // ROUND, g % ROUND)
-            quantise_w(g)
+            if g < PASSES:
+                regroup_w(g, 0, "vector")
+                regroup_w(g, 1, "vector" if g % 8 == 0 else "scalar")
+            if g + 1 < PASSES and (g + 1) >= 4 and (g + 1) % 2 == 1:
+                sort_x(g + 1)
+            if g > 0:
+                quantise_w(g - 1)
+            if g < PASSES:
+                quantise_x(g)
 
         for g in range(LEAD):
-            transpose_x(g // ROUND, g % ROUND)
+            transpose_x(g)
             prepare(g)
         for g in range(PASSES):
             if g + LEAD < PASSES:
-                transpose_x((g + LEAD) // ROUND, (g + LEAD) % ROUND)
+                transpose_x(g + LEAD)
+            elif g + LEAD < PASSES + EDGE_TYPES:
+                transpose_adj(g + LEAD - PASSES)
             support_passes(g)
-            if g + LEAD < PASSES:
+            if g + LEAD <= PASSES:
                 prepare(g + LEAD)
+            if PASSES <= g + LEAD < PASSES + EDGE_TYPES:
+                quantise_adj(g + LEAD - PASSES)
             if g == 0:
                 bias_sum = work_psum.tile([P, F_OUT], F32, tag="work")
                 nc.tensor.matmul(bias_sum[:], lhsT=ones[:], rhs=bias_row[:], start=True, stop=True)
@@ -261,40 +313,22 @@ def tile_fgg_pa_k_kernel(tc, x, adjacency_matrix, W1, b1, Wr1_words, Wr1_scales,
             if g == 9:
                 load_adj()
                 load_wr_scales()
-                for c in range(PASSES // WR_CHUNK):
-                    load_wr(c)
-            if g == PASSES - 2:
-                transpose_adj()
-                quantise_adj()
-        for g in range(PASSES):
-            residual_passes(g)
+                for c in range(4):
+                    load_wr(4 * c, 4)
+        for g in range(PASSES - 2):
+            for t in range(NODE_TILES):
+                residual_pass(g, t)
         for t in range(NODE_TILES):
-            if t % 2 == 0:
-                nc.vector.tensor_copy(out=sup_rows[:, t, :], in_=support[t][:])
-            else:
-                nc.scalar.copy(out=sup_rows[:, t, :], in_=support[t][:])
-        nc.vector.tensor_copy(
-            out=sup_grouped[:].rearrange("p (c i) t -> p c t i", i=4),
-            in_=sup_rows[:].rearrange("p t (c i) -> p c t i", i=4),
-        )
-        nc.vector.quantize_mx(
-            out=supq_codes[:].bitcast(FP8X4),
-            scales=supq_scales[:],
-            in_=sup_grouped[:].rearrange("p c t -> p (c t)"),
-        )
-
+            support_rows(t, "vector" if t % 2 == 0 else "scalar")
+        regroup_support(0)
+        regroup_support(1)
+        quantise_support(0)
+        quantise_support(1)
+        for e in range(EDGE_TYPES):
+            for t in range(NODE_TILES):
+                aggregate(e, t)
         for t in range(NODE_TILES):
-            for e in range(EDGE_TYPES):
-                n_cols = slice(e * NODES + t * P, e * NODES + (t + 1) * P)
-                f_cols = slice(e * F_OUT, (e + 1) * F_OUT)
-                nc.tensor.matmul_mx(
-                    out=total[t][:],
-                    lhsT=adjq_codes[:, n_cols].bitcast(FP8X4),
-                    lhsT_scale=adjq_scales[:, n_cols],
-                    rhs=supq_codes[:, f_cols].bitcast(FP8X4),
-                    rhs_scale=supq_scales[:, f_cols],
-                    start=False,
-                    stop=(e == EDGE_TYPES - 1),
-                )
+            for g in range(PASSES - 2, PASSES):
+                residual_pass(g, t)
             nc.vector.tensor_tensor(out=result[:, t, :], in0=total[t][:], in1=bias_f32[:], op=ADD)
             nc.sync.dma_start(out=out_view[t // 2, t % 2], in_=result[:, t, :])

from contextlib import ExitStack

import concourse.mybir as mybir
from concourse.masks import make_identity

F32 = mybir.dt.float32
BF16 = mybir.dt.bfloat16
I32 = mybir.dt.int32
U32 = mybir.dt.uint32
U8 = mybir.dt.uint8
FP8X4 = mybir.dt.float8_e4m3fn_x4
ADD = mybir.AluOpType.add

P = 128
PACK = 4
K_PASS = P * PACK
NODES = 512
FEATURES = 8192
F_OUT = 256
EDGE_TYPES = 2
NODE_TILES = NODES // P
PASSES = FEATURES // K_PASS
ROUND = 2
ROUNDS = PASSES // ROUND
W_COLS = EDGE_TYPES * F_OUT
LEAD = 2

FLOPS = 2 * NODES * FEATURES * (W_COLS + F_OUT) + 2 * EDGE_TYPES * NODES * NODES * F_OUT


def tile_fgg_pa_k_kernel(tc, x, adjacency_matrix, W1, b1, Wr1_words, Wr1_scales, out):
    nc = tc.nc
    with ExitStack() as ctx:
        ctx.enter_context(tc.manual_schedule())
        keep = ctx.enter_context(tc.tile_pool(name="keep", bufs=1))
        x_pool = ctx.enter_context(tc.tile_pool(name="x_pool", bufs=2))
        w_pool = ctx.enter_context(tc.tile_pool(name="w_pool", bufs=8))
        stage = ctx.enter_context(tc.tile_pool(name="stage", bufs=4))
        sup_psum = ctx.enter_context(tc.psum_pool(name="sup_psum", bufs=1))
        work_psum = ctx.enter_context(tc.psum_pool(name="work_psum", bufs=4))

        x_view = x.rearrange("(u p f) k -> u p f k", u=2, f=2)
        adj_view = adjacency_matrix.rearrange("e (u p f) m -> e u p (f m)", u=2, f=2)
        w1_view = W1.rearrange("e (g p j) w -> g p e (j w)", p=P, j=PACK)
        wr_view = Wr1_words.rearrange("g p n t -> p g (n t)")
        out_view = out.rearrange("(u p f) c -> u f p c", u=2, f=2)

        ident_f32 = keep.tile([P, P], F32)
        ones = keep.tile([P, P], BF16)
        xq_codes = keep.tile([P, PASSES * NODES], U32, align_bytes=64)
        xq_scales = keep.tile([P, PASSES * NODES], U8, align_bytes=64)
        wr_codes = keep.tile([P, PASSES, F_OUT], U32, align_bytes=64)
        wr_scales = keep.tile([P, PASSES, F_OUT], U8, align_bytes=64)
        adjq_codes = keep.tile([P, EDGE_TYPES * NODES], U32, align_bytes=64)
        adjq_scales = keep.tile([P, EDGE_TYPES * NODES], U8, align_bytes=64)
        sup_rows = keep.tile([P, NODE_TILES, W_COLS], BF16)
        sup_grouped = keep.tile([P, W_COLS, PACK], BF16, align_bytes=64)
        supq_codes = keep.tile([P, W_COLS], U32, align_bytes=64)
        supq_scales = keep.tile([P, W_COLS], U8, align_bytes=64)
        bias_row = keep.tile([P, F_OUT], BF16)
        bias_f32 = keep.tile([P, F_OUT], F32)
        result = keep.tile([P, NODE_TILES, F_OUT], F32)

        support = [sup_psum.tile([P, W_COLS], F32, name="support%d" % t) for t in range(NODE_TILES)]

        x_raw = {}
        x_grouped = {}
        w_raw = {}
        w_grouped = {}
        wq_codes = {}
        wq_scales = {}

        x_first = {}

        def load_first_x(i):
            x_first[i] = x_pool.tile([P, NODE_TILES, K_PASS], BF16, name="x_first", tag="x_first", bufs=ROUND)
            there = slice(i * K_PASS, (i + 1) * K_PASS)
            for u in range(2):
                nc.sync.dma_start(out=x_first[i][:, 2 * u : 2 * u + 2, :], in_=x_view[u][:, :, there])

        def load_x(r, count):
            chunk = x_pool.tile([P, NODE_TILES, count * ROUND * K_PASS], BF16, name="x_raw%d" % count, tag="x_raw%d" % count, bufs=4)
            there = slice(ROUND * r * K_PASS, ROUND * (r + count) * K_PASS)
            for u in range(2):
                nc.sync.dma_start(out=chunk[:, 2 * u : 2 * u + 2, :], in_=x_view[u][:, :, there])
            for n in range(count):
                x_raw[r + n] = chunk[:, :, n * ROUND * K_PASS : (n + 1) * ROUND * K_PASS]

        def load_w(g):
            w_raw[g] = w_pool.tile([P, EDGE_TYPES, PACK * F_OUT], BF16, name="w_raw")
            nc.sync.dma_start(out=w_raw[g][:], in_=w1_view[g])

        def load_wr(first, count):
            here = slice(first, first + count)
            nc.sync.dma_start(out=wr_codes[:, here, :].bitcast(I32), in_=wr_view[:, here, :].bitcast(I32))

        def load_wr_scales():
            for row in range(4):
                nc.sync.dma_start(
                    out=wr_scales[row:P:32, :, :].bitcast(I32),
                    in_=Wr1_scales[:, row:16:4, :].rearrange("g q n -> q g n").bitcast(I32),
                )

        adj_raw = {}

        def load_adj():
            adj_raw[0] = x_pool.tile([P, EDGE_TYPES * NODE_TILES, NODES], BF16, name="adj_raw", tag="x_raw1", bufs=4)
            for e in range(EDGE_TYPES):
                for u in range(2):
                    first = e * NODE_TILES + 2 * u
                    nc.sync.dma_start(
                        out=adj_raw[0][:, first : first + 2, :].rearrange("p f m -> p (f m)"),
                        in_=adj_view[e, u],
                    )

        x_sorted = {}

        def sort_x(g):
            r, i = g // ROUND, g % ROUND
            x_sorted[g] = stage.tile([P, NODE_TILES, K_PASS], BF16, name="x_sorted", tag="x_sorted", bufs=3)
            nc.vector.tensor_copy(
                out=x_sorted[g][:].bitcast(F32).rearrange("p t (u w) -> p t u w", u=2),
                in_=x_raw[r].bitcast(F32)[:, :, 256 * i : 256 * (i + 1)].rearrange("p t (w u) -> p t u w", u=2),
            )

        def transpose_x(g):
            r, i = g // ROUND, g % ROUND
            x_grouped[g] = stage.tile([P, NODES, PACK], BF16, name="x_grouped", tag="x_grouped", bufs=4, align_bytes=64)
            for half in range(2):
                xt = work_psum.tile([P, 2, 2 * P], F32, tag="work")
                for u in range(2):
                    for a in range(2):
                        t = 2 * half + a
                        if g in x_sorted:
                            words = x_sorted[g][:].bitcast(F32)[:, t, P * u : P * (u + 1)]
                        elif r == 0:
                            words = x_first[i][:].bitcast(F32)[:, t, u:256:2]
                        else:
                            words = x_raw[r].bitcast(F32)[:, t, 256 * i + u : 256 * (i + 1) : 2]
                        nc.tensor.transpose(xt[:, u, a * P : (a + 1) * P], words, ident_f32[:])
                nc.scalar.copy(
                    out=x_grouped[g][:].bitcast(F32)[:, 2 * P * half : 2 * P * (half + 1), :],
                    in_=xt[:].rearrange("p u n -> p n u"),
                )

        def quantise_x(g):
            nc.vector.quantize_mx(
                out=xq_codes[:, g * NODES : (g + 1) * NODES].bitcast(FP8X4),
                scales=xq_scales[:, g * NODES : (g + 1) * NODES],
                in_=x_grouped[g][:].rearrange("p n t -> p (n t)"),
            )

        def x_operand(g, t):
            cols = slice(g * NODES + t * P, g * NODES + (t + 1) * P)
            return xq_codes[:, cols].bitcast(FP8X4), xq_scales[:, cols]

        def regroup_w(g, e, engine):
            if g not in w_grouped:
                w_grouped[g] = stage.tile([P, EDGE_TYPES, F_OUT * PACK], BF16, name="w_grouped", align_bytes=64)
            src = w_raw[g][:, e, :].rearrange("p (j c i) -> p c j i", j=PACK, i=4)
            dst = w_grouped[g][:, e, :].rearrange("p (c i j) -> p c j i", j=PACK, i=4)
            if engine == "scalar":
                nc.scalar.copy(out=dst, in_=src)
            else:
                nc.vector.tensor_copy(out=dst, in_=src)

        def quantise_w(g):
            wq_codes[g] = stage.tile([P, W_COLS], U32, name="wq_codes", align_bytes=64)
            wq_scales[g] = stage.tile([P, W_COLS], U8, name="wq_scales", align_bytes=64)
            nc.vector.quantize_mx(
                out=wq_codes[g][:].bitcast(FP8X4),
                scales=wq_scales[g][:],
                in_=w_grouped[g][:].rearrange("p e n -> p (e n)"),
            )

        def support_passes(g):
            for t in range(NODE_TILES):
                codes, scales = x_operand(g, t)
                nc.tensor.matmul_mx(
                    out=support[t][:],
                    lhsT=codes,
                    lhsT_scale=scales,
                    rhs=wq_codes[g][:].bitcast(FP8X4),
                    rhs_scale=wq_scales[g][:],
                    start=(g == 0),
                    stop=(g == PASSES - 1),
                )

        total = {}

        def residual_pass(g, t):
            if g == 0:
                total[t] = work_psum.tile([P, F_OUT], F32, tag="work", name="total%d" % t)
            codes, scales = x_operand(g, t)
            nc.tensor.matmul_mx(
                out=total[t][:],
                lhsT=codes,
                lhsT_scale=scales,
                rhs=wr_codes[:, g, :].bitcast(FP8X4),
                rhs_scale=wr_scales[:, g, :],
                start=(g == 0),
                stop=(g == PASSES - 1),
            )

        def aggregate(e, t):
            n_cols = slice(e * NODES + t * P, e * NODES + (t + 1) * P)
            f_cols = slice(e * F_OUT, (e + 1) * F_OUT)
            nc.tensor.matmul_mx(
                out=total[t][:],
                lhsT=adjq_codes[:, n_cols].bitcast(FP8X4),
                lhsT_scale=adjq_scales[:, n_cols],
                rhs=supq_codes[:, f_cols].bitcast(FP8X4),
                rhs_scale=supq_scales[:, f_cols],
                start=False,
                stop=False,
            )

        adj_grouped = {}

        def transpose_adj(e):
            adj_grouped[e] = stage.tile([P, NODES, PACK], BF16, name="adj_grouped", tag="x_grouped", bufs=4, align_bytes=64)
            words = adj_raw[0][:].bitcast(F32)
            for half in range(2):
                at = work_psum.tile([P, 2, 2 * P], F32, tag="work")
                for u in range(2):
                    for a in range(2):
                        nc.tensor.transpose(
                            at[:, u, a * P : (a + 1) * P],
                            words[:, e * NODE_TILES + 2 * half + a, P * u : P * (u + 1)],
                            ident_f32[:],
                        )
                nc.scalar.copy(
                    out=adj_grouped[e][:].bitcast(F32)[:, 2 * P * half : 2 * P * (half + 1), :],
                    in_=at[:].rearrange("p u n -> p n u"),
                )

        def quantise_adj(e):
            nodes = slice(e * NODES, (e + 1) * NODES)
            nc.vector.quantize_mx(
                out=adjq_codes[:, nodes].bitcast(FP8X4),
                scales=adjq_scales[:, nodes],
                in_=adj_grouped[e][:].rearrange("p n t -> p (n t)"),
            )

        def support_rows(t, engine):
            if engine == "scalar":
                nc.scalar.copy(out=sup_rows[:, t, :], in_=support[t][:])
            else:
                nc.vector.tensor_copy(out=sup_rows[:, t, :], in_=support[t][:])

        def regroup_support(e):
            f_cols = slice(e * F_OUT, (e + 1) * F_OUT)
            nc.vector.tensor_copy(
                out=sup_grouped[:, f_cols, :].rearrange("p (c i) t -> p c t i", i=4),
                in_=sup_rows[:, :, f_cols].rearrange("p t (c i) -> p c t i", i=4),
            )

        def quantise_support(e):
            f_cols = slice(e * F_OUT, (e + 1) * F_OUT)
            nc.vector.quantize_mx(
                out=supq_codes[:, f_cols].bitcast(FP8X4),
                scales=supq_scales[:, f_cols],
                in_=sup_grouped[:, f_cols, :].rearrange("p c t -> p (c t)"),
            )

        load_first_x(0)
        load_w(0)
        load_first_x(1)
        load_w(1)
        make_identity(nc, ident_f32[:])
        nc.vector.memset(wr_scales[:].rearrange("p g n -> p (g n)").bitcast(I32), 0)
        nc.vector.memset(bias_row[:], 0.0)
        nc.vector.memset(ones[:], 1.0)
        nc.sync.dma_start(out=bias_row[0:1, :], in_=b1.unsqueeze(0))
        for r in (1, 2, 3):
            load_x(r, 1)
            load_w(ROUND * r)
            load_w(ROUND * r + 1)

        def prepare(g):
            if g < PASSES:
                regroup_w(g, 0, "vector")
                regroup_w(g, 1, "vector" if g % 8 == 0 else "scalar")
            if g + 1 < PASSES and (g + 1) >= 4 and (g + 1) % 2 == 1:
                sort_x(g + 1)
            if g > 0:
                quantise_w(g - 1)
            if g < PASSES:
                quantise_x(g)

        for g in range(LEAD):
            transpose_x(g)
            prepare(g)
        for g in range(PASSES):
            if g + LEAD < PASSES:
                transpose_x(g + LEAD)
            elif g + LEAD < PASSES + EDGE_TYPES:
                transpose_adj(g + LEAD - PASSES)
            support_passes(g)
            if g + LEAD <= PASSES:
                prepare(g + LEAD)
            if PASSES <= g + LEAD < PASSES + EDGE_TYPES:
                quantise_adj(g + LEAD - PASSES)
            if g == 0:
                bias_sum = work_psum.tile([P, F_OUT], F32, tag="work")
                nc.tensor.matmul(bias_sum[:], lhsT=ones[:], rhs=bias_row[:], start=True, stop=True)
                nc.scalar.copy(out=bias_f32[:], in_=bias_sum[:])
            if g % ROUND == 1 and g // ROUND + 4 < ROUNDS:
                r = g // ROUND + 4
                load_x(r, 1)
                load_w(ROUND * r)
                load_w(ROUND * r + 1)
            if g == 9:
                load_adj()
                load_wr_scales()
                for c in range(4):
                    load_wr(4 * c, 4)
        for g in range(PASSES - 2):
            for t in range(NODE_TILES):
                residual_pass(g, t)
        for t in range(NODE_TILES):
            support_rows(t, "vector" if t % 2 == 0 else "scalar")
        regroup_support(0)
        regroup_support(1)
        quantise_support(0)
        quantise_support(1)
        for e in range(EDGE_TYPES):
            for t in range(NODE_TILES):
                aggregate(e, t)
        for t in range(NODE_TILES):
            for g in range(PASSES - 2, PASSES):
                residual_pass(g, t)
            nc.vector.tensor_tensor(out=result[:, t, :], in0=total[t][:], in1=bias_f32[:], op=ADD)
            nc.sync.dma_start(out=out_view[t // 2, t % 2], in_=result[:, t, :])
